import numpy as np
import ml_dtypes


def mxq(x, axis, fmt="e4m3"):
    dtype, down = {"e4m3": (ml_dtypes.float8_e4m3fn, 7), "e5m2": (ml_dtypes.float8_e5m2, 14)}[fmt]
    v = np.moveaxis(np.asarray(x, np.float32).astype(ml_dtypes.bfloat16).astype(np.float64), axis, -1)
    blocks = v.reshape(v.shape[:-1] + (-1, 32))
    amax = np.abs(blocks).max(-1, keepdims=True)
    byte = np.maximum(np.where(amax > 0, np.frexp(amax)[1] - 1 + 127, 0) - down, 1)
    scale = np.exp2(byte - 127.0)
    codes = (blocks / scale).astype(np.float32).astype(dtype).astype(np.float64)
    return np.moveaxis((codes * scale).reshape(v.shape), -1, axis)


WIDE = False


def mx_kscale(k):
    if not WIDE:
        return np.ones(k)
    levels = np.array([10, -10, 5, -5, 0])
    a = np.random.permutation(np.resize(levels, k // 512 * 4)).reshape(k // 512, 4)
    idx = np.arange(k)
    return np.exp2(a[idx // 512, idx % 128 // 32])


BF16 = ml_dtypes.bfloat16


def bf(x):
    return np.asarray(x, np.float32).astype(BF16)


def f64(x):
    return np.asarray(x).astype(np.float64)


N, K, F, NB = 1024, 512, 384, 32


def setup_inputs():
    s = mx_kscale(N)
    c = s / s.min()
    r = s.max() / s
    edge = np.random.random_sample((N, N)) < NB / N
    return {"h_ln": bf(np.random.standard_normal((N, F)) * r[:, None]),
            "adj": bf(np.random.random_sample((N, N)) * edge * c[None, :]),
            "W2": bf(np.random.standard_normal((F, F)) * 2.0 / np.sqrt(F)),
            "b2": bf(np.random.standard_normal(F) * 0.2)}


def reference(h_ln, adj, W2, b2):
    a = f64(adj)
    h = f64(h_ln) @ f64(W2) + f64(b2)
    deg = a.sum(axis=1) + 1.0
    dinv = np.where(deg > 0, deg ** -0.5, 0.0)
    hs = dinv[:, None] * h
    agg = (mxq(a, 1, "e4m3") @ mxq(hs, 0, "e4m3")) + hs
    return dinv[:, None] * agg

@@ -1,0 +1,214 @@
+import concourse.mybir as mybir
+from concourse.masks import make_identity
+
+F32 = mybir.dt.float32
+BF16 = mybir.dt.bfloat16
+U32 = mybir.dt.uint32
+U8 = mybir.dt.uint8
+FP8X4 = mybir.dt.float8_e4m3fn_x4
+ALU = mybir.AluOpType
+ACT = mybir.ActivationFunctionType
+
+P = 128
+NODES = 1024
+FEAT = 384
+K_BLOCKS = FEAT // P
+PAIR = 2
+CHUNKS = NODES // (P * PAIR)
+TILES = CHUNKS * PAIR
+PACK = 4
+PASSES = NODES // (P * PACK)
+HALVES = PACK // PAIR
+FEAT_PARTS = ((0, 256), (256, 128))
+
+FLOPS = 2 * NODES * FEAT * FEAT + 2 * NODES * NODES * FEAT
+
+
+def tile_gcnlayer_pb_kernel(tc, h_ln, adj, W2, b2, out):
+    nc = tc.nc
+
+    h_rows = h_ln.rearrange("(a p e) k -> p a e k", p=P, e=PAIR)
+    adj_rows = adj.rearrange("(a p e) j -> p a e j", p=P, e=PAIR)
+    out_rows = out.rearrange("(a p e) f -> p a e f", p=P, e=PAIR)
+
+    with (
+        tc.tile_pool(name="keep", bufs=1) as keep,
+        tc.psum_pool(name="psum", bufs=2) as psum,
+    ):
+        h_sb = keep.tile([P, CHUNKS, PAIR, FEAT], BF16)
+        w_sb = keep.tile([P, K_BLOCKS, FEAT], BF16)
+        adj_sb = keep.tile([P, CHUNKS, PAIR, NODES], BF16)
+        bias_sb = keep.tile([P, FEAT], BF16)
+        ident_bf = keep.tile([P, P], BF16)
+        ident_f32 = keep.tile([P, P], F32)
+        one = keep.tile([P, 1], F32)
+        warm = keep.tile([P, 1], F32)
+        hT_sb = keep.tile([P, CHUNKS, PAIR, K_BLOCKS, P], BF16)
+        hb = keep.tile([P, TILES, FEAT], F32)
+        row_sum_sb = keep.tile([P, PAIR, 8], F32)
+        sum_scratch = keep.tile([P, CHUNKS, PAIR, NODES], BF16)
+        root = keep.tile([P, TILES], F32)
+        dinv = keep.tile([P, TILES], F32)
+        adj_grouped = keep.tile([P, TILES, PASSES, P, PACK], BF16, align_bytes=64)
+        adj_codes = keep.tile([P, TILES, PASSES, P], U32, align_bytes=64)
+        adj_scales = keep.tile([P, TILES, PASSES, P], U8, align_bytes=64)
+        hs_grouped = keep.tile([P, PASSES, FEAT, PACK], BF16, align_bytes=64)
+        hs_codes = keep.tile([P, PASSES, FEAT], U32, align_bytes=64)
+        hs_scales = keep.tile([P, PASSES, FEAT], U8, align_bytes=64)
+        agg_plus_hs = keep.tile([P, TILES, FEAT], F32)
+        out_sb = keep.tile([P, TILES, FEAT], F32)
+
+        adj_words = adj_sb[:].bitcast(F32)
+        adj_grouped_words = adj_grouped[:].bitcast(F32)
+
+        def load_adj(a):
+            nc.sync.dma_start(out=adj_sb[:, a], in_=adj_rows[:, a])
+
+        def load_h(g):
+            two = slice(g * HALVES, (g + 1) * HALVES)
+            nc.sync.dma_start(out=h_sb[:, two], in_=h_rows[:, two])
+
+        def row_sum(n):
+            a, e = divmod(n, PAIR)
+            if e == 0:
+                nc.vector.tensor_scalar(
+                    out=sum_scratch[:, a, e, :],
+                    in0=adj_sb[:, a, e, :],
+                    scalar1=1.0,
+                    scalar2=None,
+                    op0=ALU.mult,
+                    op1=ALU.add,
+                    accum_out=row_sum_sb[:, e, a : a + 1],
+                )
+            else:
+                nc.scalar.activation(
+                    out=sum_scratch[:, a, e, :],
+                    in_=adj_sb[:, a, e, :],
+                    func=ACT.Copy,
+                    accum_out=row_sum_sb[:, e, a : a + 1],
+                )
+
+        def root_of_degree(a):
+            pair = slice(a * PAIR, (a + 1) * PAIR)
+            nc.scalar.activation(
+                out=root[:, pair], in_=row_sum_sb[:, :, a], func=ACT.Sqrt, bias=1.0
+            )
+
+        def transpose_adj(n):
+            adjT_ps = psum.tile([P, PASSES * HALVES, P], F32)
+            for b in range(PASSES * HALVES):
+                nc.tensor.transpose(
+                    adjT_ps[:, b, :],
+                    adj_words[:, n // PAIR, n % PAIR, b * P : (b + 1) * P],
+                    ident_f32[:],
+                )
+            nc.scalar.copy(
+                out=adj_grouped_words[:, n],
+                in_=adjT_ps[:].rearrange("p (g u) i -> p g i u", u=HALVES),
+            )
+
+        def quantise_adj(a):
+            pair = slice(a * PAIR, (a + 1) * PAIR)
+            nc.vector.quantize_mx(
+                out=adj_codes[:, pair].rearrange("p n g i -> p (n g i)").bitcast(FP8X4),
+                scales=adj_scales[:, pair].rearrange("p n g i -> p (n g i)"),
+                in_=adj_grouped[:, pair].rearrange("p n g i t -> p (n g i t)"),
+            )
+
+        def transpose_h(a):
+            hT_ps = psum.tile([P, PAIR, K_BLOCKS, P], BF16, tag="rotating", bufs=4)
+            for e in range(PAIR):
+                for kb in range(K_BLOCKS):
+                    nc.tensor.transpose(
+                        hT_ps[:, e, kb, :], h_sb[:, a, e, kb * P : (kb + 1) * P], ident_bf[:]
+                    )
+            nc.scalar.copy(out=hT_sb[:, a], in_=hT_ps[:])
+
+        def linear(n):
+            h_ps = psum.tile([P, FEAT], F32)
+            for kb in range(K_BLOCKS):
+                nc.tensor.matmul(
+                    h_ps[:],
+                    lhsT=hT_sb[:, n // PAIR, n % PAIR, kb, :],
+                    rhs=w_sb[:, kb, :],
+                    start=(kb == 0),
+                    stop=(kb == K_BLOCKS - 1),
+                )
+            nc.vector.tensor_tensor(out=hb[:, n, :], in0=h_ps[:], in1=bias_sb[:], op=ALU.add)
+
+        def quantise_hs(g):
+            four = slice(g * PACK, (g + 1) * PACK)
+            nc.vector.reciprocal(out=dinv[:, four], in_=root[:, four])
+            for f0, width in FEAT_PARTS:
+                nc.vector.tensor_tensor(
+                    out=hs_grouped[:, g, f0 : f0 + width, :],
+                    in0=hb[:, four, f0 : f0 + width].rearrange("p t f -> p f t"),
+                    in1=dinv[:, four].unsqueeze(1).to_broadcast([P, width, PACK]),
+                    op=ALU.mult,
+                )
+            for f0, width in FEAT_PARTS:
+                nc.vector.quantize_mx(
+                    out=hs_codes[:, g, f0 : f0 + width].bitcast(FP8X4),
+                    scales=hs_scales[:, g, f0 : f0 + width],
+                    in_=hs_grouped[:, g, f0 : f0 + width, :].rearrange("p f t -> p (f t)"),
+                )
+
+        def aggregate(n):
+            agg_ps = psum.tile([P, FEAT], F32, tag="rotating", bufs=4)
+            for f0, width in FEAT_PARTS:
+                for g in range(PASSES):
+                    nc.tensor.matmul_mx(
+                        out=agg_ps[:, f0 : f0 + width],
+                        lhsT=adj_codes[:, n, g, :].bitcast(FP8X4),
+                        lhsT_scale=adj_scales[:, n, g, :],
+                        rhs=hs_codes[:, g, f0 : f0 + width].bitcast(FP8X4),
+                        rhs_scale=hs_scales[:, g, f0 : f0 + width],
+                        start=(g == 0),
+                        stop=(g == PASSES - 1),
+                    )
+            nc.vector.scalar_tensor_tensor(
+                out=agg_plus_hs[:, n, :],
+                in0=hb[:, n, :],
+                scalar=dinv[:, n : n + 1],
+                in1=agg_ps[:],
+                op0=ALU.mult,
+                op1=ALU.add,
+            )
+            nc.scalar.activation(
+                out=out_sb[:, n, :],
+                in_=agg_plus_hs[:, n, :],
+                func=ACT.Copy,
+                scale=dinv[:, n : n + 1],
+            )
+            nc.sync.dma_start(out=out_rows[:, n // PAIR, n % PAIR, :], in_=out_sb[:, n, :])
+
+        with tc.manual_schedule():
+            nc.scalar.dma_start(out=bias_sb[:], in_=b2.partition_broadcast(P))
+            load_h(0)
+            load_adj(0)
+            nc.sync.dma_start(out=w_sb[:], in_=W2.rearrange("(kb p) f -> p kb f", p=P))
+            load_adj(1)
+            load_h(1)
+            load_adj(2)
+            load_adj(3)
+            make_identity(nc, ident_bf[:])
+            make_identity(nc, ident_f32[:])
+            nc.vector.memset(one[:], 1.0)
+            nc.scalar.sqrt(out=warm[:], in_=one[:])
+
+            for g in range(PASSES):
+                chunks = range(g * HALVES, (g + 1) * HALVES)
+                for a in chunks:
+                    transpose_h(a)
+                for a in chunks:
+                    row_sum(a * PAIR)
+                    transpose_adj(a * PAIR)
+                    transpose_adj(a * PAIR + 1)
+                    row_sum(a * PAIR + 1)
+                    root_of_degree(a)
+                    linear(a * PAIR)
+                    linear(a * PAIR + 1)
+                    quantise_adj(a)
+                quantise_hs(g)
+            for n in range(TILES):
+                aggregate(n)

@@ -38,7 +38,9 @@ def tile_gcnlayer_pb_kernel(tc, h_ln, adj, W2, b2, out):
         h_sb = keep.tile([P, CHUNKS, PAIR, FEAT], BF16)
         w_sb = keep.tile([P, K_BLOCKS, FEAT], BF16)
         adj_sb = keep.tile([P, CHUNKS, PAIR, NODES], BF16)
-        bias_sb = keep.tile([P, FEAT], BF16)
+        bias_rows = keep.tile([P, FEAT], BF16)
+        ones_bf = keep.tile([P, P], BF16)
+        bias_sb = keep.tile([P, FEAT], F32)
         ident_bf = keep.tile([P, P], BF16)
         ident_f32 = keep.tile([P, P], F32)
         one = keep.tile([P, 1], F32)
@@ -67,6 +69,11 @@ def tile_gcnlayer_pb_kernel(tc, h_ln, adj, W2, b2, out):
         def load_h(g):
             two = slice(g * HALVES, (g + 1) * HALVES)
             nc.sync.dma_start(out=h_sb[:, two], in_=h_rows[:, two])
+
+        def spread_bias():
+            bias_ps = psum.tile([P, FEAT], F32, tag="rotating", bufs=4)
+            nc.tensor.matmul(bias_ps[:], lhsT=ones_bf[:], rhs=bias_rows[:], start=True, stop=True)
+            nc.scalar.copy(out=bias_sb[:], in_=bias_ps[:])
 
         def row_sum(n):
             a, e = divmod(n, PAIR)
@@ -183,7 +190,9 @@ def tile_gcnlayer_pb_kernel(tc, h_ln, adj, W2, b2, out):
             nc.sync.dma_start(out=out_rows[:, n // PAIR, n % PAIR, :], in_=out_sb[:, n, :])
 
         with tc.manual_schedule():
-            nc.scalar.dma_start(out=bias_sb[:], in_=b2.partition_broadcast(P))
+            nc.vector.memset(bias_rows[:], 0.0)
+            nc.vector.memset(ones_bf[:], 1.0)
+            nc.scalar.dma_start(out=bias_rows[0:1, :], in_=b2.unsqueeze(0))
             load_h(0)
             load_adj(0)
             nc.sync.dma_start(out=w_sb[:], in_=W2.rearrange("(kb p) f -> p kb f", p=P))
@@ -200,6 +209,8 @@ def tile_gcnlayer_pb_kernel(tc, h_ln, adj, W2, b2, out):
                 chunks = range(g * HALVES, (g + 1) * HALVES)
                 for a in chunks:
                     transpose_h(a)
+                if g == 0:
+                    spread_bias()
                 for a in chunks:
                     row_sum(a * PAIR)
                     transpose_adj(a * PAIR)

@@ -3,6 +3,7 @@ from concourse.masks import make_identity
 
 F32 = mybir.dt.float32
 BF16 = mybir.dt.bfloat16
+I32 = mybir.dt.int32
 U32 = mybir.dt.uint32
 U8 = mybir.dt.uint8
 FP8X4 = mybir.dt.float8_e4m3fn_x4
@@ -19,7 +20,9 @@ TILES = CHUNKS * PAIR
 PACK = 4
 PASSES = NODES // (P * PACK)
 HALVES = PACK // PAIR
+MX_COLS = 512
 FEAT_PARTS = ((0, 256), (256, 128))
+BANKS = 8
 
 FLOPS = 2 * NODES * FEAT * FEAT + 2 * NODES * NODES * FEAT
 
@@ -33,7 +36,7 @@ def tile_gcnlayer_pb_kernel(tc, h_ln, adj, W2, b2, out):
 
     with (
         tc.tile_pool(name="keep", bufs=1) as keep,
-        tc.psum_pool(name="psum", bufs=2) as psum,
+        tc.psum_pool(name="psum", bufs=BANKS) as psum,
     ):
         h_sb = keep.tile([P, CHUNKS, PAIR, FEAT], BF16)
         w_sb = keep.tile([P, K_BLOCKS, FEAT], BF16)
@@ -47,21 +50,23 @@ def tile_gcnlayer_pb_kernel(tc, h_ln, adj, W2, b2, out):
         warm = keep.tile([P, 1], F32)
         hT_sb = keep.tile([P, CHUNKS, PAIR, K_BLOCKS, P], BF16)
         hb = keep.tile([P, TILES, FEAT], F32)
-        row_sum_sb = keep.tile([P, PAIR, 8], F32)
-        sum_scratch = keep.tile([P, CHUNKS, PAIR, NODES], BF16)
+        hs_self = keep.tile([P, TILES, FEAT], F32)
+        row_sums = keep.tile([P, PASSES, 8], F32)
+        sum_scratch = keep.tile([P, TILES, NODES], BF16)
         root = keep.tile([P, TILES], F32)
         dinv = keep.tile([P, TILES], F32)
+        dinv_sq = keep.tile([P, TILES], F32)
         adj_grouped = keep.tile([P, TILES, PASSES, P, PACK], BF16, align_bytes=64)
         adj_codes = keep.tile([P, TILES, PASSES, P], U32, align_bytes=64)
         adj_scales = keep.tile([P, TILES, PASSES, P], U8, align_bytes=64)
         hs_grouped = keep.tile([P, PASSES, FEAT, PACK], BF16, align_bytes=64)
-        hs_codes = keep.tile([P, PASSES, FEAT], U32, align_bytes=64)
-        hs_scales = keep.tile([P, PASSES, FEAT], U8, align_bytes=64)
-        agg_plus_hs = keep.tile([P, TILES, FEAT], F32)
+        hs_codes = keep.tile([P, PASSES, MX_COLS], U32, align_bytes=64)
+        hs_scales = keep.tile([P, PASSES, MX_COLS], U8, align_bytes=64)
         out_sb = keep.tile([P, TILES, FEAT], F32)
 
         adj_words = adj_sb[:].bitcast(F32)
         adj_grouped_words = adj_grouped[:].bitcast(F32)
+        agg_banks = {}
 
         def load_adj(a):
             nc.sync.dma_start(out=adj_sb[:, a], in_=adj_rows[:, a])
@@ -71,38 +76,39 @@ def tile_gcnlayer_pb_kernel(tc, h_ln, adj, W2, b2, out):
             nc.sync.dma_start(out=h_sb[:, two], in_=h_rows[:, two])
 
         def spread_bias():
-            bias_ps = psum.tile([P, FEAT], F32, tag="rotating", bufs=4)
+            bias_ps = psum.tile([P, FEAT], F32, tag="bank")
             nc.tensor.matmul(bias_ps[:], lhsT=ones_bf[:], rhs=bias_rows[:], start=True, stop=True)
             nc.scalar.copy(out=bias_sb[:], in_=bias_ps[:])
 
         def row_sum(n):
-            a, e = divmod(n, PAIR)
-            if e == 0:
+            g, t = divmod(n, PACK)
+            rows = adj_sb[:, n // PAIR, n % PAIR, :]
+            if g == 0:
                 nc.vector.tensor_scalar(
-                    out=sum_scratch[:, a, e, :],
-                    in0=adj_sb[:, a, e, :],
+                    out=sum_scratch[:, n, :],
+                    in0=rows,
                     scalar1=1.0,
                     scalar2=None,
                     op0=ALU.mult,
                     op1=ALU.add,
-                    accum_out=row_sum_sb[:, e, a : a + 1],
+                    accum_out=row_sums[:, g, t : t + 1],
                 )
             else:
                 nc.scalar.activation(
-                    out=sum_scratch[:, a, e, :],
-                    in_=adj_sb[:, a, e, :],
+                    out=sum_scratch[:, n, :],
+                    in_=rows,
                     func=ACT.Copy,
-                    accum_out=row_sum_sb[:, e, a : a + 1],
+                    accum_out=row_sums[:, g, t : t + 1],
                 )
 
-        def root_of_degree(a):
-            pair = slice(a * PAIR, (a + 1) * PAIR)
+        def root_of_degree(g):
+            four = slice(g * PACK, (g + 1) * PACK)
             nc.scalar.activation(
-                out=root[:, pair], in_=row_sum_sb[:, :, a], func=ACT.Sqrt, bias=1.0
+                out=root[:, four], in_=row_sums[:, g, 0:PACK], func=ACT.Sqrt, bias=1.0
             )
 
         def transpose_adj(n):
-            adjT_ps = psum.tile([P, PASSES * HALVES, P], F32)
+            adjT_ps = psum.tile([P, PASSES * HALVES, P], F32, tag="bank")
             for b in range(PASSES * HALVES):
                 nc.tensor.transpose(
                     adjT_ps[:, b, :],
@@ -123,7 +129,7 @@ def tile_gcnlayer_pb_kernel(tc, h_ln, adj, W2, b2, out):
             )
 
         def transpose_h(a):
-            hT_ps = psum.tile([P, PAIR, K_BLOCKS, P], BF16, tag="rotating", bufs=4)
+            hT_ps = psum.tile([P, PAIR, K_BLOCKS, P], BF16, tag="bank")
             for e in range(PAIR):
                 for kb in range(K_BLOCKS):
                     nc.tensor.transpose(
@@ -132,7 +138,7 @@ def tile_gcnlayer_pb_kernel(tc, h_ln, adj, W2, b2, out):
             nc.scalar.copy(out=hT_sb[:, a], in_=hT_ps[:])
 
         def linear(n):
-            h_ps = psum.tile([P, FEAT], F32)
+            h_ps = psum.tile([P, FEAT], F32, tag="bank")
             for kb in range(K_BLOCKS):
                 nc.tensor.matmul(
                     h_ps[:],
@@ -160,66 +166,100 @@ def tile_gcnlayer_pb_kernel(tc, h_ln, adj, W2, b2, out):
                     in_=hs_grouped[:, g, f0 : f0 + width, :].rearrange("p f t -> p (f t)"),
                 )
 
-        def aggregate(n):
-            agg_ps = psum.tile([P, FEAT], F32, tag="rotating", bufs=4)
-            for f0, width in FEAT_PARTS:
-                for g in range(PASSES):
-                    nc.tensor.matmul_mx(
-                        out=agg_ps[:, f0 : f0 + width],
-                        lhsT=adj_codes[:, n, g, :].bitcast(FP8X4),
-                        lhsT_scale=adj_scales[:, n, g, :],
-                        rhs=hs_codes[:, g, f0 : f0 + width].bitcast(FP8X4),
-                        rhs_scale=hs_scales[:, g, f0 : f0 + width],
-                        start=(g == 0),
-                        stop=(g == PASSES - 1),
-                    )
+        def self_terms(g):
+            four = slice(g * PACK, (g + 1) * PACK)
+            nc.scalar.square(out=dinv_sq[:, four], in_=dinv[:, four])
+            for n in range(g * PACK, (g + 1) * PACK):
+                nc.scalar.activation(
+                    out=hs_self[:, n, :],
+                    in_=hb[:, n, :],
+                    func=ACT.Copy,
+                    scale=dinv_sq[:, n : n + 1],
+                )
+
+        def aggregate(n, g):
+            if g == 0:
+                agg_banks[n] = psum.tile([P, MX_COLS], F32, tag="bank", name="agg_ps")
+            nc.tensor.matmul_mx(
+                out=agg_banks[n][:],
+                lhsT=adj_codes[:, n, g, :].bitcast(FP8X4),
+                lhsT_scale=adj_scales[:, n, g, :],
+                rhs=hs_codes[:, g, :].bitcast(FP8X4),
+                rhs_scale=hs_scales[:, g, :],
+                start=(g == 0),
+                stop=(g == PASSES - 1),
+            )
+
+        def finish(n):
             nc.vector.scalar_tensor_tensor(
-                out=agg_plus_hs[:, n, :],
-                in0=hb[:, n, :],
+                out=out_sb[:, n, :],
+                in0=agg_banks[n][:, 0:FEAT],
                 scalar=dinv[:, n : n + 1],
-                in1=agg_ps[:],
+                in1=hs_self[:, n, :],
                 op0=ALU.mult,
                 op1=ALU.add,
-            )
-            nc.scalar.activation(
-                out=out_sb[:, n, :],
-                in_=agg_plus_hs[:, n, :],
-                func=ACT.Copy,
-                scale=dinv[:, n : n + 1],
             )
             nc.sync.dma_start(out=out_rows[:, n // PAIR, n % PAIR, :], in_=out_sb[:, n, :])
 
         with tc.manual_schedule():
-            nc.vector.memset(bias_rows[:], 0.0)
-            nc.vector.memset(ones_bf[:], 1.0)
-            nc.scalar.dma_start(out=bias_rows[0:1, :], in_=b2.unsqueeze(0))
-            load_h(0)
+            nc.gpsimd.memset(bias_rows[:], 0.0)
+            nc.gpsimd.memset(ones_bf[:], 1.0)
             load_adj(0)
-            nc.sync.dma_start(out=w_sb[:], in_=W2.rearrange("(kb p) f -> p kb f", p=P))
+            nc.sync.dma_start(out=bias_rows[0:1, :], in_=b2.unsqueeze(0))
+            load_h(0)
             load_adj(1)
-            load_h(1)
+            nc.sync.dma_start(out=w_sb[:], in_=W2.rearrange("(kb p) f -> p kb f", p=P))
             load_adj(2)
             load_adj(3)
-            make_identity(nc, ident_bf[:])
+            load_h(1)
             make_identity(nc, ident_f32[:])
+            make_identity(nc, ident_bf[:])
             nc.vector.memset(one[:], 1.0)
             nc.scalar.sqrt(out=warm[:], in_=one[:])
+            nc.vector.memset(hs_codes[:, :, FEAT:MX_COLS].bitcast(I32), 0)
+            nc.vector.memset(hs_scales[:, :, FEAT:MX_COLS].bitcast(I32), 0)
 
+            row_sum(0)
+            row_sum(1)
+            row_sum(2)
+            transpose_adj(0)
+            transpose_adj(1)
+            quantise_adj(0)
+            row_sum(3)
+            transpose_h(0)
+            transpose_h(1)
+            spread_bias()
+            transpose_adj(2)
+            transpose_adj(3)
+            root_of_degree(0)
+            quantise_adj(1)
+            for n in range(PACK):
+                linear(n)
+            quantise_hs(0)
+
+            row_sum(4)
+            row_sum(5)
+            transpose_h(2)
+            transpose_h(3)
+            row_sum(6)
+            row_sum(7)
+            root_of_degree(1)
+            for n in range(PACK, TILES):
+                transpose_adj(n)
+            for n in range(PACK, TILES):
+                linear(n)
+            quantise_hs(1)
+            quantise_adj(2)
+            quantise_adj(3)
             for g in range(PASSES):
-                chunks = range(g * HALVES, (g + 1) * HALVES)
-                for a in chunks:
-                    transpose_h(a)
-                if g == 0:
-                    spread_bias()
-                for a in chunks:
-                    row_sum(a * PAIR)
-                    transpose_adj(a * PAIR)
-                    transpose_adj(a * PAIR + 1)
-                    row_sum(a * PAIR + 1)
-                    root_of_degree(a)
-                    linear(a * PAIR)
-                    linear(a * PAIR + 1)
-                    quantise_adj(a)
-                quantise_hs(g)
-            for n in range(TILES):
-                aggregate(n)
+                self_terms(g)
+
+            for n in range(PACK):
+                aggregate(n, 0)
+            for n in range(PACK):
+                aggregate(n, 1)
+                finish(n)
+            for n in range(PACK, TILES):
+                aggregate(n, 0)
+                aggregate(n, 1)
+                finish(n)

@@ -23,6 +23,7 @@ HALVES = PACK // PAIR
 MX_COLS = 512
 FEAT_PARTS = ((0, 256), (256, 128))
 BANKS = 8
+WARM_PASSES = 6
 
 FLOPS = 2 * NODES * FEAT * FEAT + 2 * NODES * NODES * FEAT
 
@@ -216,8 +217,19 @@ def tile_gcnlayer_pb_kernel(tc, h_ln, adj, W2, b2, out):
             make_identity(nc, ident_bf[:])
             nc.vector.memset(one[:], 1.0)
             nc.scalar.sqrt(out=warm[:], in_=one[:])
-            nc.vector.memset(hs_codes[:, :, FEAT:MX_COLS].bitcast(I32), 0)
-            nc.vector.memset(hs_scales[:, :, FEAT:MX_COLS].bitcast(I32), 0)
+            nc.vector.memset(hs_codes[:].bitcast(I32), 0)
+            nc.vector.memset(hs_scales[:].bitcast(I32), 0)
+            warm_ps = psum.tile([P, MX_COLS], F32, tag="bank")
+            for idle in range(WARM_PASSES):
+                nc.tensor.matmul_mx(
+                    out=warm_ps[:],
+                    lhsT=hs_codes[:, 1, 0:P].bitcast(FP8X4),
+                    lhsT_scale=hs_scales[:, 1, 0:P],
+                    rhs=hs_codes[:, 0, :].bitcast(FP8X4),
+                    rhs_scale=hs_scales[:, 0, :],
+                    start=True,
+                    stop=True,
+                )
 
             row_sum(0)
             row_sum(1)

@@ -23,7 +23,6 @@ HALVES = PACK // PAIR
 MX_COLS = 512
 FEAT_PARTS = ((0, 256), (256, 128))
 BANKS = 8
-WARM_PASSES = 6
 
 FLOPS = 2 * NODES * FEAT * FEAT + 2 * NODES * NODES * FEAT
 
@@ -85,11 +84,11 @@ def tile_gcnlayer_pb_kernel(tc, h_ln, adj, W2, b2, out):
             g, t = divmod(n, PACK)
             rows = adj_sb[:, n // PAIR, n % PAIR, :]
             if g == 0:
-                nc.vector.tensor_scalar(
-                    out=sum_scratch[:, n, :],
-                    in0=rows,
-                    scalar1=1.0,
-                    scalar2=None,
+                nc.vector.scalar_tensor_tensor(
+                    out=sum_scratch[:, n, :].bitcast(F32),
+                    in0=rows[:, 0 : NODES // 2],
+                    scalar=1.0,
+                    in1=rows[:, NODES // 2 : NODES],
                     op0=ALU.mult,
                     op1=ALU.add,
                     accum_out=row_sums[:, g, t : t + 1],
@@ -217,19 +216,8 @@ def tile_gcnlayer_pb_kernel(tc, h_ln, adj, W2, b2, out):
             make_identity(nc, ident_bf[:])
             nc.vector.memset(one[:], 1.0)
             nc.scalar.sqrt(out=warm[:], in_=one[:])
-            nc.vector.memset(hs_codes[:].bitcast(I32), 0)
-            nc.vector.memset(hs_scales[:].bitcast(I32), 0)
-            warm_ps = psum.tile([P, MX_COLS], F32, tag="bank")
-            for idle in range(WARM_PASSES):
-                nc.tensor.matmul_mx(
-                    out=warm_ps[:],
-                    lhsT=hs_codes[:, 1, 0:P].bitcast(FP8X4),
-                    lhsT_scale=hs_scales[:, 1, 0:P],
-                    rhs=hs_codes[:, 0, :].bitcast(FP8X4),
-                    rhs_scale=hs_scales[:, 0, :],
-                    start=True,
-                    stop=True,
-                )
+            nc.vector.memset(hs_codes[:, :, FEAT:MX_COLS].bitcast(I32), 0)
+            nc.vector.memset(hs_scales[:, :, FEAT:MX_COLS].bitcast(I32), 0)
 
             row_sum(0)
             row_sum(1)
@@ -244,9 +232,11 @@ def tile_gcnlayer_pb_kernel(tc, h_ln, adj, W2, b2, out):
             transpose_adj(2)
             transpose_adj(3)
             root_of_degree(0)
+            linear(0)
+            linear(1)
             quantise_adj(1)
-            for n in range(PACK):
-                linear(n)
+            linear(2)
+            linear(3)
             quantise_hs(0)
 
             row_sum(4)

import concourse.mybir as mybir
from concourse.masks import make_identity

F32 = mybir.dt.float32
BF16 = mybir.dt.bfloat16
I32 = mybir.dt.int32
U32 = mybir.dt.uint32
U8 = mybir.dt.uint8
FP8X4 = mybir.dt.float8_e4m3fn_x4
ALU = mybir.AluOpType
ACT = mybir.ActivationFunctionType

P = 128
NODES = 1024
FEAT = 384
K_BLOCKS = FEAT // P
PAIR = 2
CHUNKS = NODES // (P * PAIR)
TILES = CHUNKS * PAIR
PACK = 4
PASSES = NODES // (P * PACK)
HALVES = PACK // PAIR
MX_COLS = 512
FEAT_PARTS = ((0, 256), (256, 128))
BANKS = 8

FLOPS = 2 * NODES * FEAT * FEAT + 2 * NODES * NODES * FEAT


def tile_gcnlayer_pb_kernel(tc, h_ln, adj, W2, b2, out):
    nc = tc.nc

    h_rows = h_ln.rearrange("(a p e) k -> p a e k", p=P, e=PAIR)
    adj_rows = adj.rearrange("(a p e) j -> p a e j", p=P, e=PAIR)
    out_rows = out.rearrange("(a p e) f -> p a e f", p=P, e=PAIR)

    with (
        tc.tile_pool(name="keep", bufs=1) as keep,
        tc.psum_pool(name="psum", bufs=BANKS) as psum,
    ):
        h_sb = keep.tile([P, CHUNKS, PAIR, FEAT], BF16)
        w_sb = keep.tile([P, K_BLOCKS, FEAT], BF16)
        adj_sb = keep.tile([P, CHUNKS, PAIR, NODES], BF16)
        bias_rows = keep.tile([P, FEAT], BF16)
        ones_bf = keep.tile([P, P], BF16)
        bias_sb = keep.tile([P, FEAT], F32)
        ident_bf = keep.tile([P, P], BF16)
        ident_f32 = keep.tile([P, P], F32)
        one = keep.tile([P, 1], F32)
        warm = keep.tile([P, 1], F32)
        hT_sb = keep.tile([P, CHUNKS, PAIR, K_BLOCKS, P], BF16)
        hb = keep.tile([P, TILES, FEAT], F32)
        hs_self = keep.tile([P, TILES, FEAT], F32)
        row_sums = keep.tile([P, PASSES, 8], F32)
        sum_scratch = keep.tile([P, TILES, NODES], BF16)
        root = keep.tile([P, TILES], F32)
        dinv = keep.tile([P, TILES], F32)
        dinv_sq = keep.tile([P, TILES], F32)
        adj_grouped = keep.tile([P, TILES, PASSES, P, PACK], BF16, align_bytes=64)
        adj_codes = keep.tile([P, TILES, PASSES, P], U32, align_bytes=64)
        adj_scales = keep.tile([P, TILES, PASSES, P], U8, align_bytes=64)
        hs_grouped = keep.tile([P, PASSES, FEAT, PACK], BF16, align_bytes=64)
        hs_codes = keep.tile([P, PASSES, MX_COLS], U32, align_bytes=64)
        hs_scales = keep.tile([P, PASSES, MX_COLS], U8, align_bytes=64)
        out_sb = keep.tile([P, TILES, FEAT], F32)

        adj_words = adj_sb[:].bitcast(F32)
        adj_grouped_words = adj_grouped[:].bitcast(F32)
        agg_banks = {}

        def load_adj(a):
            nc.sync.dma_start(out=adj_sb[:, a], in_=adj_rows[:, a])

        def load_h(g):
            two = slice(g * HALVES, (g + 1) * HALVES)
            nc.sync.dma_start(out=h_sb[:, two], in_=h_rows[:, two])

        def spread_bias():
            bias_ps = psum.tile([P, FEAT], F32, tag="bank")
            nc.tensor.matmul(bias_ps[:], lhsT=ones_bf[:], rhs=bias_rows[:], start=True, stop=True)
            nc.scalar.copy(out=bias_sb[:], in_=bias_ps[:])

        def row_sum(n):
            g, t = divmod(n, PACK)
            rows = adj_sb[:, n // PAIR, n % PAIR, :]
            if g == 0:
                nc.vector.scalar_tensor_tensor(
                    out=sum_scratch[:, n, :].bitcast(F32),
                    in0=rows[:, 0 : NODES // 2],
                    scalar=1.0,
                    in1=rows[:, NODES // 2 : NODES],
                    op0=ALU.mult,
                    op1=ALU.add,
                    accum_out=row_sums[:, g, t : t + 1],
                )
            else:
                nc.scalar.activation(
                    out=sum_scratch[:, n, :],
                    in_=rows,
                    func=ACT.Copy,
                    accum_out=row_sums[:, g, t : t + 1],
                )

        def root_of_degree(g):
            four = slice(g * PACK, (g + 1) * PACK)
            nc.scalar.activation(
                out=root[:, four], in_=row_sums[:, g, 0:PACK], func=ACT.Sqrt, bias=1.0
            )

        def transpose_adj(n):
            adjT_ps = psum.tile([P, PASSES * HALVES, P], F32, tag="bank")
            for b in range(PASSES * HALVES):
                nc.tensor.transpose(
                    adjT_ps[:, b, :],
                    adj_words[:, n // PAIR, n % PAIR, b * P : (b + 1) * P],
                    ident_f32[:],
                )
            nc.scalar.copy(
                out=adj_grouped_words[:, n],
                in_=adjT_ps[:].rearrange("p (g u) i -> p g i u", u=HALVES),
            )

        def quantise_adj(a):
            pair = slice(a * PAIR, (a + 1) * PAIR)
            nc.vector.quantize_mx(
                out=adj_codes[:, pair].rearrange("p n g i -> p (n g i)").bitcast(FP8X4),
                scales=adj_scales[:, pair].rearrange("p n g i -> p (n g i)"),
                in_=adj_grouped[:, pair].rearrange("p n g i t -> p (n g i t)"),
            )

        def transpose_h(a):
            hT_ps = psum.tile([P, PAIR, K_BLOCKS, P], BF16, tag="bank")
            for e in range(PAIR):
                for kb in range(K_BLOCKS):
                    nc.tensor.transpose(
                        hT_ps[:, e, kb, :], h_sb[:, a, e, kb * P : (kb + 1) * P], ident_bf[:]
                    )
            nc.scalar.copy(out=hT_sb[:, a], in_=hT_ps[:])

        def linear(n):
            h_ps = psum.tile([P, FEAT], F32, tag="bank")
            for kb in range(K_BLOCKS):
                nc.tensor.matmul(
                    h_ps[:],
                    lhsT=hT_sb[:, n // PAIR, n % PAIR, kb, :],
                    rhs=w_sb[:, kb, :],
                    start=(kb == 0),
                    stop=(kb == K_BLOCKS - 1),
                )
            nc.vector.tensor_tensor(out=hb[:, n, :], in0=h_ps[:], in1=bias_sb[:], op=ALU.add)

        def quantise_hs(g):
            four = slice(g * PACK, (g + 1) * PACK)
            nc.vector.reciprocal(out=dinv[:, four], in_=root[:, four])
            for f0, width in FEAT_PARTS:
                nc.vector.tensor_tensor(
                    out=hs_grouped[:, g, f0 : f0 + width, :],
                    in0=hb[:, four, f0 : f0 + width].rearrange("p t f -> p f t"),
                    in1=dinv[:, four].unsqueeze(1).to_broadcast([P, width, PACK]),
                    op=ALU.mult,
                )
            for f0, width in FEAT_PARTS:
                nc.vector.quantize_mx(
                    out=hs_codes[:, g, f0 : f0 + width].bitcast(FP8X4),
                    scales=hs_scales[:, g, f0 : f0 + width],
                    in_=hs_grouped[:, g, f0 : f0 + width, :].rearrange("p f t -> p (f t)"),
                )

        def self_terms(g):
            four = slice(g * PACK, (g + 1) * PACK)
            nc.scalar.square(out=dinv_sq[:, four], in_=dinv[:, four])
            for n in range(g * PACK, (g + 1) * PACK):
                nc.scalar.activation(
                    out=hs_self[:, n, :],
                    in_=hb[:, n, :],
                    func=ACT.Copy,
                    scale=dinv_sq[:, n : n + 1],
                )

        def aggregate(n, g):
            if g == 0:
                agg_banks[n] = psum.tile([P, MX_COLS], F32, tag="bank", name="agg_ps")
            nc.tensor.matmul_mx(
                out=agg_banks[n][:],
                lhsT=adj_codes[:, n, g, :].bitcast(FP8X4),
                lhsT_scale=adj_scales[:, n, g, :],
                rhs=hs_codes[:, g, :].bitcast(FP8X4),
                rhs_scale=hs_scales[:, g, :],
                start=(g == 0),
                stop=(g == PASSES - 1),
            )

        def finish(n):
            nc.vector.scalar_tensor_tensor(
                out=out_sb[:, n, :],
                in0=agg_banks[n][:, 0:FEAT],
                scalar=dinv[:, n : n + 1],
                in1=hs_self[:, n, :],
                op0=ALU.mult,
                op1=ALU.add,
            )
            nc.sync.dma_start(out=out_rows[:, n // PAIR, n % PAIR, :], in_=out_sb[:, n, :])

        with tc.manual_schedule():
            nc.gpsimd.memset(bias_rows[:], 0.0)
            nc.gpsimd.memset(ones_bf[:], 1.0)
            load_adj(0)
            nc.sync.dma_start(out=bias_rows[0:1, :], in_=b2.unsqueeze(0))
            load_h(0)
            load_adj(1)
            nc.sync.dma_start(out=w_sb[:], in_=W2.rearrange("(kb p) f -> p kb f", p=P))
            load_adj(2)
            load_adj(3)
            load_h(1)
            make_identity(nc, ident_f32[:])
            make_identity(nc, ident_bf[:])
            nc.vector.memset(one[:], 1.0)
            nc.scalar.sqrt(out=warm[:], in_=one[:])
            nc.vector.memset(hs_codes[:, :, FEAT:MX_COLS].bitcast(I32), 0)
            nc.vector.memset(hs_scales[:, :, FEAT:MX_COLS].bitcast(I32), 0)

            row_sum(0)
            row_sum(1)
            row_sum(2)
            transpose_adj(0)
            transpose_adj(1)
            quantise_adj(0)
            row_sum(3)
            transpose_h(0)
            transpose_h(1)
            spread_bias()
            transpose_adj(2)
            transpose_adj(3)
            root_of_degree(0)
            linear(0)
            linear(1)
            quantise_adj(1)
            linear(2)
            linear(3)
            quantise_hs(0)

            row_sum(4)
            row_sum(5)
            transpose_h(2)
            transpose_h(3)
            row_sum(6)
            row_sum(7)
            root_of_degree(1)
            for n in range(PACK, TILES):
                transpose_adj(n)
            for n in range(PACK, TILES):
                linear(n)
            quantise_hs(1)
            quantise_adj(2)
            quantise_adj(3)
            for g in range(PASSES):
                self_terms(g)

            for n in range(PACK):
                aggregate(n, 0)
            for n in range(PACK):
                aggregate(n, 1)
                finish(n)
            for n in range(PACK, TILES):
                aggregate(n, 0)
                aggregate(n, 1)
                finish(n)
